import numpy as np
import ml_dtypes

BF16 = ml_dtypes.bfloat16


def bf(x):
    return np.asarray(x, np.float32).astype(BF16)


def f32(x):
    return np.asarray(x, np.float32)


def f64(x):
    return np.asarray(x).astype(np.float64)


def striped(idx):
    return np.tile(idx.reshape(-1, 16).T, (8, 1))


C, S, N = 128, 4096, 128
SCORE_STD = 3.0


def sigmoid(v):
    return 1.0 / (1.0 + np.exp(-v))


def setup_inputs():
    return {"u": bf(np.random.standard_normal((C, S))), "h": bf(SCORE_STD / np.sqrt(C) * np.random.standard_normal((C, N))), "offs": striped(np.random.permutation(np.tile(np.arange(S), 2))[:N])}


def reference(u, h, offs):
    idx = offs[:16].T.reshape(-1)
    uu = f64(u)
    hh = f64(h)
    pos = -np.log(sigmoid((uu[:, idx] * hh).sum(axis=0)))
    neg = np.log(sigmoid(-(hh.T @ uu)).sum(axis=1))
    return np.mean(pos + neg, keepdims=True)[None, :]

@@ -1,0 +1,77 @@
+import concourse.mybir as mybir
+
+BF16, F32, U16 = mybir.dt.bfloat16, mybir.dt.float32, mybir.dt.uint16
+FUNC = mybir.ActivationFunctionType
+ALU = mybir.AluOpType
+AXIS = mybir.AxisListType
+
+C, S, N = 128, 4096, 128
+BANK = 512
+CHUNKS = S // BANK
+
+FLOPS = 2 * C * S * N + 2 * C * N
+
+
+def tile_cbow_kernel(tc, u, h, offs, out):
+    nc = tc.nc
+    with (
+        tc.tile_pool(name="held", bufs=1) as held,
+        tc.tile_pool(name="unread", bufs=2) as unread,
+        tc.psum_pool(name="banks", bufs=4) as banks,
+        tc.psum_pool(name="small", bufs=1) as small,
+    ):
+        offsets = held.tile([128, N // 16], U16, name="offsets")
+        nc.sync.dma_start(offsets[:], offs)
+        h_bf = held.tile([C, N], BF16, name="h_bf")
+        nc.scalar.dma_start(h_bf[:], h)
+        u_bf = held.tile([C, S], BF16, name="u_bf")
+        for k in range(CHUNKS):
+            cols = slice(k * BANK, (k + 1) * BANK)
+            nc.sync.dma_start(u_bf[:, cols], u[:, cols])
+
+        ones = held.tile([C, 1], F32, name="ones")
+        nc.vector.memset(ones[:], 1.0)
+        mean_weights = held.tile([N, 1], F32, name="mean_weights")
+        nc.vector.memset(mean_weights[:], 1.0 / N)
+        h_f32 = held.tile([C, N], F32, name="h_f32")
+        nc.vector.tensor_copy(h_f32[:], h_bf[:])
+
+        u_f32 = held.tile([C, S], F32, name="u_f32")
+        neg_parts = held.tile([N, CHUNKS], F32, name="neg_parts")
+        for k in range(CHUNKS):
+            cols = slice(k * BANK, (k + 1) * BANK)
+            scores = banks.tile([N, BANK], F32, name="scores")
+            nc.tensor.matmul(scores[:], h_bf[:], u_bf[:, cols], start=True, stop=True)
+            sigmoids = unread.tile([N, BANK], BF16, name="sigmoids")
+            nc.scalar.activation(
+                sigmoids[:], scores[:], FUNC.Sigmoid, scale=-1.0, accum_out=neg_parts[:, k : k + 1]
+            )
+            nc.vector.tensor_copy(u_f32[:, cols], u_bf[:, cols])
+
+        picked = held.tile([C, N], F32, name="picked")
+        nc.vector.tensor_tensor(picked[:], u_f32[:].indirect(offsets[:]), h_f32[:], ALU.mult)
+        target = small.tile([N, 1], F32, name="target")
+        nc.tensor.matmul(target[:], picked[:], ones[:], start=True, stop=True)
+
+        minus_target = held.tile([N, 1], F32, name="minus_target")
+        nc.vector.tensor_scalar_mul(minus_target[:], target[:], -1.0)
+        abs_target = held.tile([N, 1], F32, name="abs_target")
+        nc.vector.tensor_tensor(abs_target[:], target[:], minus_target[:], ALU.max)
+        hinge = held.tile([N, 1], F32, name="hinge")
+        nc.vector.tensor_scalar_max(hinge[:], minus_target[:], 0.0)
+        sig_abs = held.tile([N, 1], F32, name="sig_abs")
+        nc.scalar.activation(sig_abs[:], abs_target[:], FUNC.Sigmoid)
+        inv_sig_abs = held.tile([N, 1], F32, name="inv_sig_abs")
+        nc.vector.reciprocal(inv_sig_abs[:], sig_abs[:])
+
+        neg_sum = held.tile([N, 1], F32, name="neg_sum")
+        nc.vector.reduce_sum(neg_sum[:], neg_parts[:], axis=AXIS.X)
+        log_term = held.tile([N, 1], F32, name="log_term")
+        nc.scalar.activation(log_term[:], neg_sum[:], FUNC.Ln, scale=inv_sig_abs[:])
+
+        mean = small.tile([1, 1], F32, name="mean")
+        nc.tensor.matmul(mean[:], mean_weights[:], hinge[:], start=True, stop=False)
+        nc.tensor.matmul(mean[:], mean_weights[:], log_term[:], start=False, stop=True)
+        result = held.tile([1, 1], F32, name="result")
+        nc.vector.tensor_copy(result[:], mean[:])
+        nc.sync.dma_start(out, result[:])

@@ -1,4 +1,5 @@
 import concourse.mybir as mybir
+from concourse.masks import make_identity
 
 BF16, F32, U16 = mybir.dt.bfloat16, mybir.dt.float32, mybir.dt.uint16
 FUNC = mybir.ActivationFunctionType
@@ -33,6 +34,8 @@ def tile_cbow_kernel(tc, u, h, offs, out):
         nc.vector.memset(ones[:], 1.0)
         mean_weights = held.tile([N, 1], F32, name="mean_weights")
         nc.vector.memset(mean_weights[:], 1.0 / N)
+        identity = held.tile([N, N], F32, name="identity")
+        make_identity(nc, identity[:])
         h_f32 = held.tile([C, N], F32, name="h_f32")
         nc.vector.tensor_copy(h_f32[:], h_bf[:])
 
@@ -64,14 +67,20 @@ def tile_cbow_kernel(tc, u, h, offs, out):
         inv_sig_abs = held.tile([N, 1], F32, name="inv_sig_abs")
         nc.vector.reciprocal(inv_sig_abs[:], sig_abs[:])
 
+        hinge_mean_psum = small.tile([1, 1], F32, name="hinge_mean_psum")
+        nc.tensor.matmul(hinge_mean_psum[:], mean_weights[:], hinge[:], start=True, stop=True)
+        hinge_mean = held.tile([1, 1], F32, name="hinge_mean")
+        nc.vector.tensor_copy(hinge_mean[:], hinge_mean_psum[:])
+
         neg_sum = held.tile([N, 1], F32, name="neg_sum")
         nc.vector.reduce_sum(neg_sum[:], neg_parts[:], axis=AXIS.X)
-        log_term = held.tile([N, 1], F32, name="log_term")
-        nc.scalar.activation(log_term[:], neg_sum[:], FUNC.Ln, scale=inv_sig_abs[:])
-
-        mean = small.tile([1, 1], F32, name="mean")
-        nc.tensor.matmul(mean[:], mean_weights[:], hinge[:], start=True, stop=False)
-        nc.tensor.matmul(mean[:], mean_weights[:], log_term[:], start=False, stop=True)
+        ratio = held.tile([N, 1], F32, name="ratio")
+        nc.vector.tensor_tensor(ratio[:], neg_sum[:], inv_sig_abs[:], ALU.mult)
+        ratio_row = small.tile([1, N], F32, name="ratio_row")
+        nc.tensor.transpose(ratio_row[:], ratio[:], identity[:])
+        logs = held.tile([1, N], F32, name="logs")
+        log_sum = held.tile([1, 1], F32, name="log_sum")
+        nc.scalar.activation(logs[:], ratio_row[:], FUNC.Ln, accum_out=log_sum[:])
         result = held.tile([1, 1], F32, name="result")
-        nc.vector.tensor_copy(result[:], mean[:])
+        nc.scalar.activation(result[:], log_sum[:], FUNC.Identity, scale=1.0 / N, bias=hinge_mean[:])
         nc.sync.dma_start(out, result[:])

@@ -1,5 +1,4 @@
 import concourse.mybir as mybir
-from concourse.masks import make_identity
 
 BF16, F32, U16 = mybir.dt.bfloat16, mybir.dt.float32, mybir.dt.uint16
 FUNC = mybir.ActivationFunctionType
@@ -8,46 +7,48 @@ AXIS = mybir.AxisListType
 
 C, S, N = 128, 4096, 128
 BANK = 512
-CHUNKS = S // BANK
+WIDTHS = [BANK // 4, BANK // 4, BANK // 2] + [BANK] * (S // BANK - 1)
 
 FLOPS = 2 * C * S * N + 2 * C * N
 
 
 def tile_cbow_kernel(tc, u, h, offs, out):
     nc = tc.nc
+    pieces = [slice(sum(WIDTHS[:k]), sum(WIDTHS[: k + 1])) for k in range(len(WIDTHS))]
     with (
         tc.tile_pool(name="held", bufs=1) as held,
         tc.tile_pool(name="unread", bufs=2) as unread,
         tc.psum_pool(name="banks", bufs=4) as banks,
         tc.psum_pool(name="small", bufs=1) as small,
     ):
-        offsets = held.tile([128, N // 16], U16, name="offsets")
-        nc.sync.dma_start(offsets[:], offs)
         h_bf = held.tile([C, N], BF16, name="h_bf")
         nc.scalar.dma_start(h_bf[:], h)
         u_bf = held.tile([C, S], BF16, name="u_bf")
-        for k in range(CHUNKS):
-            cols = slice(k * BANK, (k + 1) * BANK)
+        for cols in pieces:
             nc.sync.dma_start(u_bf[:, cols], u[:, cols])
+        offsets = held.tile([128, N // 16], U16, name="offsets")
+        nc.sync.dma_start(offsets[:], offs)
 
         ones = held.tile([C, 1], F32, name="ones")
         nc.vector.memset(ones[:], 1.0)
         mean_weights = held.tile([N, 1], F32, name="mean_weights")
         nc.vector.memset(mean_weights[:], 1.0 / N)
-        identity = held.tile([N, N], F32, name="identity")
-        make_identity(nc, identity[:])
         h_f32 = held.tile([C, N], F32, name="h_f32")
         nc.vector.tensor_copy(h_f32[:], h_bf[:])
 
         u_f32 = held.tile([C, S], F32, name="u_f32")
-        neg_parts = held.tile([N, CHUNKS], F32, name="neg_parts")
-        for k in range(CHUNKS):
-            cols = slice(k * BANK, (k + 1) * BANK)
+        neg_parts = held.tile([N, len(pieces)], F32, name="neg_parts")
+        for k, cols in enumerate(pieces):
+            width = WIDTHS[k]
             scores = banks.tile([N, BANK], F32, name="scores")
-            nc.tensor.matmul(scores[:], h_bf[:], u_bf[:, cols], start=True, stop=True)
+            nc.tensor.matmul(scores[:, :width], h_bf[:], u_bf[:, cols], start=True, stop=True)
             sigmoids = unread.tile([N, BANK], BF16, name="sigmoids")
             nc.scalar.activation(
-                sigmoids[:], scores[:], FUNC.Sigmoid, scale=-1.0, accum_out=neg_parts[:, k : k + 1]
+                sigmoids[:, :width],
+                scores[:, :width],
+                FUNC.Sigmoid,
+                scale=-1.0,
+                accum_out=neg_parts[:, k : k + 1],
             )
             nc.vector.tensor_copy(u_f32[:, cols], u_bf[:, cols])
 
@@ -67,20 +68,14 @@ def tile_cbow_kernel(tc, u, h, offs, out):
         inv_sig_abs = held.tile([N, 1], F32, name="inv_sig_abs")
         nc.vector.reciprocal(inv_sig_abs[:], sig_abs[:])
 
-        hinge_mean_psum = small.tile([1, 1], F32, name="hinge_mean_psum")
-        nc.tensor.matmul(hinge_mean_psum[:], mean_weights[:], hinge[:], start=True, stop=True)
-        hinge_mean = held.tile([1, 1], F32, name="hinge_mean")
-        nc.vector.tensor_copy(hinge_mean[:], hinge_mean_psum[:])
-
         neg_sum = held.tile([N, 1], F32, name="neg_sum")
         nc.vector.reduce_sum(neg_sum[:], neg_parts[:], axis=AXIS.X)
-        ratio = held.tile([N, 1], F32, name="ratio")
-        nc.vector.tensor_tensor(ratio[:], neg_sum[:], inv_sig_abs[:], ALU.mult)
-        ratio_row = small.tile([1, N], F32, name="ratio_row")
-        nc.tensor.transpose(ratio_row[:], ratio[:], identity[:])
-        logs = held.tile([1, N], F32, name="logs")
-        log_sum = held.tile([1, 1], F32, name="log_sum")
-        nc.scalar.activation(logs[:], ratio_row[:], FUNC.Ln, accum_out=log_sum[:])
+        log_term = held.tile([N, 1], F32, name="log_term")
+        nc.scalar.activation(log_term[:], neg_sum[:], FUNC.Ln, scale=inv_sig_abs[:])
+
+        mean = small.tile([1, 1], F32, name="mean")
+        nc.tensor.matmul(mean[:], mean_weights[:], hinge[:], start=True, stop=False)
+        nc.tensor.matmul(mean[:], mean_weights[:], log_term[:], start=False, stop=True)
         result = held.tile([1, 1], F32, name="result")
-        nc.scalar.activation(result[:], log_sum[:], FUNC.Identity, scale=1.0 / N, bias=hinge_mean[:])
+        nc.vector.tensor_copy(result[:], mean[:])
         nc.sync.dma_start(out, result[:])

@@ -8,6 +8,7 @@ AXIS = mybir.AxisListType
 C, S, N = 128, 4096, 128
 BANK = 512
 WIDTHS = [BANK // 4, BANK // 4, BANK // 2] + [BANK] * (S // BANK - 1)
+WARM_UP_MATMULS = 4
 
 FLOPS = 2 * C * S * N + 2 * C * N
 
@@ -28,6 +29,12 @@ def tile_cbow_kernel(tc, u, h, offs, out):
             nc.sync.dma_start(u_bf[:, cols], u[:, cols])
         offsets = held.tile([128, N // 16], U16, name="offsets")
         nc.sync.dma_start(offsets[:], offs)
+
+        zeros = held.tile([C, BANK], BF16, name="zeros")
+        nc.vector.memset(zeros[:], 0.0)
+        warm_up = small.tile([N, BANK], F32, name="warm_up")
+        for repeat in range(WARM_UP_MATMULS):
+            nc.tensor.matmul(warm_up[:], zeros[:, :N], zeros[:], start=True, stop=True)
 
         ones = held.tile([C, 1], F32, name="ones")
         nc.vector.memset(ones[:], 1.0)

@@ -1,9 +1,9 @@
 import concourse.mybir as mybir
+from concourse.masks import make_identity
 
 BF16, F32, U16 = mybir.dt.bfloat16, mybir.dt.float32, mybir.dt.uint16
 FUNC = mybir.ActivationFunctionType
 ALU = mybir.AluOpType
-AXIS = mybir.AxisListType
 
 C, S, N = 128, 4096, 128
 BANK = 512
@@ -40,6 +40,8 @@ def tile_cbow_kernel(tc, u, h, offs, out):
         nc.vector.memset(ones[:], 1.0)
         mean_weights = held.tile([N, 1], F32, name="mean_weights")
         nc.vector.memset(mean_weights[:], 1.0 / N)
+        identity = held.tile([N, N], F32, name="identity")
+        make_identity(nc, identity[:])
         h_f32 = held.tile([C, N], F32, name="h_f32")
         nc.vector.tensor_copy(h_f32[:], h_bf[:])
 
@@ -75,14 +77,22 @@ def tile_cbow_kernel(tc, u, h, offs, out):
         inv_sig_abs = held.tile([N, 1], F32, name="inv_sig_abs")
         nc.vector.reciprocal(inv_sig_abs[:], sig_abs[:])
 
-        neg_sum = held.tile([N, 1], F32, name="neg_sum")
-        nc.vector.reduce_sum(neg_sum[:], neg_parts[:], axis=AXIS.X)
-        log_term = held.tile([N, 1], F32, name="log_term")
-        nc.scalar.activation(log_term[:], neg_sum[:], FUNC.Ln, scale=inv_sig_abs[:])
+        hinge_mean_psum = small.tile([1, 1], F32, name="hinge_mean_psum")
+        nc.tensor.matmul(hinge_mean_psum[:], mean_weights[:], hinge[:], start=True, stop=True)
+        hinge_mean = held.tile([1, 1], F32, name="hinge_mean")
+        nc.vector.tensor_copy(hinge_mean[:], hinge_mean_psum[:])
 
-        mean = small.tile([1, 1], F32, name="mean")
-        nc.tensor.matmul(mean[:], mean_weights[:], hinge[:], start=True, stop=False)
-        nc.tensor.matmul(mean[:], mean_weights[:], log_term[:], start=False, stop=True)
+        scaled_parts = held.tile([N, len(pieces)], F32, name="scaled_parts")
+        ratio = held.tile([N, 1], F32, name="ratio")
+        nc.vector.tensor_scalar(
+            scaled_parts[:], neg_parts[:], inv_sig_abs[:], None, ALU.mult, ALU.add, accum_out=ratio[:]
+        )
+        ratio_row = small.tile([1, N], F32, name="ratio_row")
+        nc.tensor.matmul(ratio_row[:], ratio[:], identity[:], start=True, stop=True)
+        logs = held.tile([1, N], F32, name="logs")
+        log_sum = held.tile([1, 1], F32, name="log_sum")
+        nc.scalar.activation(logs[:], ratio_row[:], FUNC.Ln, accum_out=log_sum[:])
+
         result = held.tile([1, 1], F32, name="result")
-        nc.vector.tensor_copy(result[:], mean[:])
-        nc.sync.dma_start(out, result[:])
+        nc.scalar.activation(result[:], log_sum[:], FUNC.Identity, bias=hinge_mean[:], scale=1.0 / N)
+        nc.scalar.dma_start(out, result[:])

@@ -88,11 +88,11 @@ def tile_cbow_kernel(tc, u, h, offs, out):
             scaled_parts[:], neg_parts[:], inv_sig_abs[:], None, ALU.mult, ALU.add, accum_out=ratio[:]
         )
         ratio_row = small.tile([1, N], F32, name="ratio_row")
-        nc.tensor.matmul(ratio_row[:], ratio[:], identity[:], start=True, stop=True)
+        nc.tensor.transpose(ratio_row[:], ratio[:], identity[:])
         logs = held.tile([1, N], F32, name="logs")
         log_sum = held.tile([1, 1], F32, name="log_sum")
         nc.scalar.activation(logs[:], ratio_row[:], FUNC.Ln, accum_out=log_sum[:])
 
         result = held.tile([1, 1], F32, name="result")
         nc.scalar.activation(result[:], log_sum[:], FUNC.Identity, bias=hinge_mean[:], scale=1.0 / N)
-        nc.scalar.dma_start(out, result[:])
+        nc.sync.dma_start(out, result[:])

@@ -8,7 +8,7 @@ ALU = mybir.AluOpType
 C, S, N = 128, 4096, 128
 BANK = 512
 WIDTHS = [BANK // 4, BANK // 4, BANK // 2] + [BANK] * (S // BANK - 1)
-WARM_UP_MATMULS = 4
+WARM_UP_MATMULS = 2
 
 FLOPS = 2 * C * S * N + 2 * C * N
 

@@ -23,7 +23,7 @@ def tile_cbow_kernel(tc, u, h, offs, out):
         tc.psum_pool(name="small", bufs=1) as small,
     ):
         h_bf = held.tile([C, N], BF16, name="h_bf")
-        nc.scalar.dma_start(h_bf[:], h)
+        nc.sync.dma_start(h_bf[:], h)
         u_bf = held.tile([C, S], BF16, name="u_bf")
         for cols in pieces:
             nc.sync.dma_start(u_bf[:, cols], u[:, cols])

@@ -41,7 +41,8 @@ def tile_cbow_kernel(tc, u, h, offs, out):
         mean_weights = held.tile([N, 1], F32, name="mean_weights")
         nc.vector.memset(mean_weights[:], 1.0 / N)
         identity = held.tile([N, N], F32, name="identity")
-        make_identity(nc, identity[:])
+        nc.vector.memset(identity[:], 0.0)
+        make_identity(nc, identity[:], nomemset=True)
         h_f32 = held.tile([C, N], F32, name="h_f32")
         nc.vector.tensor_copy(h_f32[:], h_bf[:])
 

import concourse.mybir as mybir
from concourse.masks import make_identity

BF16, F32, U16 = mybir.dt.bfloat16, mybir.dt.float32, mybir.dt.uint16
FUNC = mybir.ActivationFunctionType
ALU = mybir.AluOpType

C, S, N = 128, 4096, 128
BANK = 512
WIDTHS = [BANK // 4, BANK // 4, BANK // 2] + [BANK] * (S // BANK - 1)
WARM_UP_MATMULS = 2

FLOPS = 2 * C * S * N + 2 * C * N


def tile_cbow_kernel(tc, u, h, offs, out):
    nc = tc.nc
    pieces = [slice(sum(WIDTHS[:k]), sum(WIDTHS[: k + 1])) for k in range(len(WIDTHS))]
    with (
        tc.tile_pool(name="held", bufs=1) as held,
        tc.tile_pool(name="unread", bufs=2) as unread,
        tc.psum_pool(name="banks", bufs=4) as banks,
        tc.psum_pool(name="small", bufs=1) as small,
    ):
        h_bf = held.tile([C, N], BF16, name="h_bf")
        nc.sync.dma_start(h_bf[:], h)
        u_bf = held.tile([C, S], BF16, name="u_bf")
        for cols in pieces:
            nc.sync.dma_start(u_bf[:, cols], u[:, cols])
        offsets = held.tile([128, N // 16], U16, name="offsets")
        nc.sync.dma_start(offsets[:], offs)

        zeros = held.tile([C, BANK], BF16, name="zeros")
        nc.vector.memset(zeros[:], 0.0)
        warm_up = small.tile([N, BANK], F32, name="warm_up")
        for repeat in range(WARM_UP_MATMULS):
            nc.tensor.matmul(warm_up[:], zeros[:, :N], zeros[:], start=True, stop=True)

        ones = held.tile([C, 1], F32, name="ones")
        nc.vector.memset(ones[:], 1.0)
        mean_weights = held.tile([N, 1], F32, name="mean_weights")
        nc.vector.memset(mean_weights[:], 1.0 / N)
        identity = held.tile([N, N], F32, name="identity")
        nc.vector.memset(identity[:], 0.0)
        make_identity(nc, identity[:], nomemset=True)
        h_f32 = held.tile([C, N], F32, name="h_f32")
        nc.vector.tensor_copy(h_f32[:], h_bf[:])

        u_f32 = held.tile([C, S], F32, name="u_f32")
        neg_parts = held.tile([N, len(pieces)], F32, name="neg_parts")
        for k, cols in enumerate(pieces):
            width = WIDTHS[k]
            scores = banks.tile([N, BANK], F32, name="scores")
            nc.tensor.matmul(scores[:, :width], h_bf[:], u_bf[:, cols], start=True, stop=True)
            sigmoids = unread.tile([N, BANK], BF16, name="sigmoids")
            nc.scalar.activation(
                sigmoids[:, :width],
                scores[:, :width],
                FUNC.Sigmoid,
                scale=-1.0,
                accum_out=neg_parts[:, k : k + 1],
            )
            nc.vector.tensor_copy(u_f32[:, cols], u_bf[:, cols])

        picked = held.tile([C, N], F32, name="picked")
        nc.vector.tensor_tensor(picked[:], u_f32[:].indirect(offsets[:]), h_f32[:], ALU.mult)
        target = small.tile([N, 1], F32, name="target")
        nc.tensor.matmul(target[:], picked[:], ones[:], start=True, stop=True)

        minus_target = held.tile([N, 1], F32, name="minus_target")
        nc.vector.tensor_scalar_mul(minus_target[:], target[:], -1.0)
        abs_target = held.tile([N, 1], F32, name="abs_target")
        nc.vector.tensor_tensor(abs_target[:], target[:], minus_target[:], ALU.max)
        hinge = held.tile([N, 1], F32, name="hinge")
        nc.vector.tensor_scalar_max(hinge[:], minus_target[:], 0.0)
        sig_abs = held.tile([N, 1], F32, name="sig_abs")
        nc.scalar.activation(sig_abs[:], abs_target[:], FUNC.Sigmoid)
        inv_sig_abs = held.tile([N, 1], F32, name="inv_sig_abs")
        nc.vector.reciprocal(inv_sig_abs[:], sig_abs[:])

        hinge_mean_psum = small.tile([1, 1], F32, name="hinge_mean_psum")
        nc.tensor.matmul(hinge_mean_psum[:], mean_weights[:], hinge[:], start=True, stop=True)
        hinge_mean = held.tile([1, 1], F32, name="hinge_mean")
        nc.vector.tensor_copy(hinge_mean[:], hinge_mean_psum[:])

        scaled_parts = held.tile([N, len(pieces)], F32, name="scaled_parts")
        ratio = held.tile([N, 1], F32, name="ratio")
        nc.vector.tensor_scalar(
            scaled_parts[:], neg_parts[:], inv_sig_abs[:], None, ALU.mult, ALU.add, accum_out=ratio[:]
        )
        ratio_row = small.tile([1, N], F32, name="ratio_row")
        nc.tensor.transpose(ratio_row[:], ratio[:], identity[:])
        logs = held.tile([1, N], F32, name="logs")
        log_sum = held.tile([1, 1], F32, name="log_sum")
        nc.scalar.activation(logs[:], ratio_row[:], FUNC.Ln, accum_out=log_sum[:])

        result = held.tile([1, 1], F32, name="result")
        nc.scalar.activation(result[:], log_sum[:], FUNC.Identity, bias=hinge_mean[:], scale=1.0 / N)
        nc.sync.dma_start(out, result[:])
